import numpy as np
import ml_dtypes


def mxq(x, axis, fmt="e4m3"):
    dtype, down = {"e4m3": (ml_dtypes.float8_e4m3fn, 7), "e5m2": (ml_dtypes.float8_e5m2, 14)}[fmt]
    v = np.moveaxis(np.asarray(x, np.float32).astype(ml_dtypes.bfloat16).astype(np.float64), axis, -1)
    blocks = v.reshape(v.shape[:-1] + (-1, 32))
    amax = np.abs(blocks).max(-1, keepdims=True)
    byte = np.maximum(np.where(amax > 0, np.frexp(amax)[1] - 1 + 127, 0) - down, 1)
    scale = np.exp2(byte - 127.0)
    codes = (blocks / scale).astype(np.float32).astype(dtype).astype(np.float64)
    return np.moveaxis((codes * scale).reshape(v.shape), -1, axis)


WIDE = False


def mx_kscale(k):
    if not WIDE:
        return np.ones(k)
    levels = np.array([10, -10, 5, -5, 0])
    if k % 512:
        return np.exp2(np.random.permutation(np.resize(levels, k // 32))).repeat(32)
    a = np.empty((k // 512, 16))
    for p in range(k // 512):
        a[p, :8] = np.random.permutation(np.resize(levels, 8))
        for g in range(8):
            far = levels[np.abs(levels - a[p, g]) >= 10]
            a[p, g + 8] = far[np.random.randint(len(far))]
    return np.exp2(a.ravel()).repeat(32)


BF16 = ml_dtypes.bfloat16


def bf(x):
    return np.asarray(x, np.float32).astype(BF16)


def f64(x):
    return np.asarray(x).astype(np.float64)


B, D, H = 4096, 512, 512
C = D + H
EPS = 1e-3


def sigmoid(v):
    return 1.0 / (1.0 + np.exp(-v))


def layer_norm(v, gamma, beta):
    m = v.mean(-1, keepdims=True)
    var = v.var(-1, keepdims=True)
    return (v - m) / np.sqrt(var + EPS) * gamma + beta


def setup_inputs():
    s = mx_kscale(D)
    t = mx_kscale(H)
    w_u = np.random.standard_normal((C, H)) / np.sqrt(C)
    w_u[:D] = w_u[:D] / s[:, None]
    g = np.random.standard_normal((B, H))
    return {"x": bf(np.random.standard_normal((B, D)) * s),
            "hidden_state": bf(np.random.standard_normal((B, H))),
            "swiglu": bf(g / (1.0 + np.exp(-g)) * np.random.standard_normal((B, H))),
            "W_u": bf(w_u),
            "b_u": bf(np.random.standard_normal(H) * 0.3),
            "gamma_h": bf((1.0 + 0.1 * np.random.standard_normal(H)) * t),
            "beta_h": bf(0.1 * np.random.standard_normal(H) * t),
            "W_d": bf(np.random.standard_normal((H, D)) / np.sqrt(H) / t[:, None]),
            "b_d": bf(np.random.standard_normal(D) * 0.3),
            "gamma_o": bf(1.0 + 0.1 * np.random.standard_normal(D)),
            "beta_o": bf(0.1 * np.random.standard_normal(D))}


def reference(x, hidden_state, swiglu, W_u, b_u, gamma_h, beta_h, W_d, b_d, gamma_o, beta_o):
    h = f64(hidden_state)
    combined = np.concatenate([f64(x), h], axis=-1)
    u = sigmoid((mxq(combined, 1, "e4m3") @ mxq(f64(W_u), 0, "e4m3")) + f64(b_u))
    new_h = layer_norm((1.0 - u) * h + u * f64(swiglu) + h, f64(gamma_h), f64(beta_h))
    out = layer_norm((mxq(new_h, 1, "e4m3") @ mxq(f64(W_d), 0, "e4m3")) + f64(b_d), f64(gamma_o), f64(beta_o))
    return out, new_h

@@ -1,0 +1,421 @@
+from contextlib import ExitStack
+
+import concourse.mybir as mybir
+from concourse.masks import make_identity
+
+F32 = mybir.dt.float32
+BF16 = mybir.dt.bfloat16
+U32 = mybir.dt.uint32
+U8 = mybir.dt.uint8
+FP8X4 = mybir.dt.float8_e4m3fn_x4
+ALU = mybir.AluOpType
+ACT = mybir.ActivationFunctionType
+
+P = 128
+PACK = 4
+B, D, H = 4096, 512, 512
+EPS = 1e-3
+CHUNKS = H // P
+SUB = 2
+TOK = SUB * P
+GROUPS = B // TOK
+BANK = 512
+CPB = BANK // TOK
+LOOKAHEAD = 3
+
+FLOPS = 2 * B * (D + H) * H + 2 * B * H * D
+
+
+def quantise_weight(nc, pool, keep, raw, passes, width, label, deal):
+    quads = pool.tile([P, passes, width, PACK], BF16, align_bytes=64, name=label + "_quads", bufs=1)
+    for c in range(passes):
+        if deal:
+            nc.vector.tensor_copy(
+                out=quads[:, c].rearrange("p (c m) t -> p c m t", c=CHUNKS),
+                in_=raw[:, c].rearrange("p t (m c) -> p c m t", c=CHUNKS),
+            )
+        else:
+            nc.vector.tensor_copy(out=quads[:, c], in_=raw[:, c].rearrange("p t n -> p n t"))
+    codes = keep.tile([P, passes, width], U32, align_bytes=64, name=label + "_codes")
+    scales = keep.tile([P, passes, width], U8, align_bytes=64, name=label + "_scales")
+    nc.vector.quantize_mx(
+        out=codes[:].rearrange("p c n -> p (c n)").bitcast(FP8X4),
+        scales=scales[:].rearrange("p c n -> p (c n)"),
+        in_=quads[:].rearrange("p c n t -> p (c n t)"),
+    )
+    return codes, scales
+
+
+def tile_recurrentffn_pb_t_kernel(
+    tc, x, hidden_state, swiglu, W_u, b_u, gamma_h, beta_h, W_d, b_d, gamma_o, beta_o, out_0, out_1
+):
+    nc = tc.nc
+    x_v = x.rearrange("(p j) d -> p j d", p=P)
+    h_v = hidden_state.rearrange("(p j) d -> p j d", p=P)
+    s_v = swiglu.rearrange("(p j) d -> p j d", p=P)
+    out_v = out_0.rearrange("(p j) d -> p j d", p=P)
+    newh_v = out_1.rearrange("(p j) d -> p j d", p=P)
+
+    with ExitStack() as ctx:
+        ctx.enter_context(tc.manual_schedule())
+        keep = ctx.enter_context(tc.tile_pool(name="keep", bufs=1))
+        hold = ctx.enter_context(tc.tile_pool(name="hold", bufs=GROUPS))
+        inp = ctx.enter_context(tc.tile_pool(name="inp", bufs=4))
+        early = ctx.enter_context(tc.tile_pool(name="early", bufs=2))
+        stat = ctx.enter_context(tc.tile_pool(name="stat", bufs=8))
+        psum = ctx.enter_context(tc.psum_pool(name="psum", bufs=8))
+
+        live = {}
+
+        def group_rows(g):
+            return slice(g * SUB, (g + 1) * SUB)
+
+        def load_gate_inputs(g):
+            x_sb = inp.tile([P, SUB, D], BF16, bufs=3)
+            nc.sync.dma_start(out=x_sb[:], in_=x_v[:, group_rows(g), :])
+            h_sb = inp.tile([P, SUB, H], BF16, bufs=6)
+            nc.sync.dma_start(out=h_sb[:], in_=h_v[:, group_rows(g), :])
+            live["x", g], live["h", g] = x_sb, h_sb
+
+        def load_candidate(g):
+            s_sb = inp.tile([P, SUB, H], BF16, bufs=4)
+            nc.sync.dma_start(out=s_sb[:], in_=s_v[:, group_rows(g), :])
+            live["s", g] = s_sb
+
+        ident = keep.tile([P, P], F32)
+        make_identity(nc, ident[:])
+        eps_col = keep.tile([P, 1], F32)
+        nc.gpsimd.memset(eps_col[:], EPS)
+
+        def turn_inputs(g):
+            for t in range(SUB):
+                xhT = psum.tile([P, 2, 2, P], F32, tag="bank")
+                for c, src in enumerate((live["x", g], live["h", g])):
+                    src_words = src[:, t, :].bitcast(F32)
+                    for u in range(2):
+                        nc.tensor.transpose(xhT[:, c, u, :], src_words[:, u : 2 * P : 2], ident[:])
+                live["xhT", g, t] = xhT
+
+        with tc.tile_pool(name="prep", bufs=1) as prep:
+            load_gate_inputs(0)
+            wu_raw = prep.tile([P, 2, PACK, H], BF16)
+            wu_v = W_u.rearrange("(c p t) n -> c p t n", c=2, p=P)
+            for c in range(2):
+                nc.sync.dma_start(out=wu_raw[:, c], in_=wu_v[c])
+            load_candidate(0)
+            for g in range(1, LOOKAHEAD):
+                load_gate_inputs(g)
+                load_candidate(g)
+            turn_inputs(0)
+
+            vec_raw = prep.tile([P, 3, 16], BF16)
+            for v, vec in enumerate((b_u, gamma_h, beta_h)):
+                nc.gpsimd.dma_start(out=vec_raw[:, v, :CHUNKS], in_=vec.rearrange("(p c) -> p c", c=CHUNKS))
+            vec_cols = keep.tile([P, 3, CHUNKS], F32)
+            nc.gpsimd.tensor_copy(out=vec_cols[:], in_=vec_raw[:, :, :CHUNKS])
+            wu_codes, wu_scales = quantise_weight(nc, prep, keep, wu_raw, 2, H, "wu", True)
+
+        def column(v, m):
+            return vec_cols[:, v, m : m + 1]
+
+        late = ctx.enter_context(tc.tile_pool(name="late", bufs=2))
+
+        wd_raw = late.tile([P, 1, PACK, D], BF16, bufs=1)
+        nc.gpsimd.dma_start(out=wd_raw[:, 0], in_=W_d.rearrange("(p m) n -> p m n", p=P))
+        bd_all = keep.tile([P, D], BF16)
+        nc.gpsimd.dma_start(out=bd_all[:], in_=b_d.partition_broadcast(P))
+        ones = keep.tile([P, P], BF16)
+        nc.gpsimd.memset(ones[:], 1.0)
+        first_rows = late.tile([P, 2, D], BF16, bufs=1)
+        nc.gpsimd.memset(first_rows[:], 0.0)
+        nc.gpsimd.dma_start(out=first_rows[0:1, 0, :], in_=gamma_o.rearrange("(o d) -> o d", o=1))
+        nc.gpsimd.dma_start(out=first_rows[0:1, 1, :], in_=beta_o.rearrange("(o d) -> o d", o=1))
+
+        def prepare_second_half():
+            live["wd"] = quantise_weight(nc, late, keep, wd_raw, 1, D, "wd", False)
+            go_all = psum.tile([P, D], F32, tag="bank")
+            nc.tensor.matmul(out=go_all[:], lhsT=ones[:], rhs=first_rows[:, 0, :], start=True, stop=True)
+            bo_all = psum.tile([P, D], F32, tag="bank")
+            nc.tensor.matmul(out=bo_all[:], lhsT=ones[:], rhs=first_rows[:, 1, :], start=True, stop=True)
+            live["go_all"], live["bo_all"] = go_all, bo_all
+
+        def copy_inputs_out(g):
+            xh_quads = early.tile([P, 2 * TOK * PACK], BF16, align_bytes=64)
+            xh_words = xh_quads[:].bitcast(F32).rearrange("q (c k u) -> q c k u", c=2, u=2)
+            for t in range(SUB):
+                nc.scalar.copy(
+                    out=xh_words[:, :, t * P : (t + 1) * P, :],
+                    in_=live["xhT", g, t][:].rearrange("q c u k -> q c k u"),
+                )
+            live["xh_quads", g] = xh_quads
+
+        def quantise_inputs(g):
+            xh_codes = early.tile([P, 2, TOK], U32, align_bytes=64)
+            xh_scales = early.tile([P, 2, TOK], U8, align_bytes=64)
+            nc.vector.quantize_mx(
+                out=xh_codes[:].rearrange("q c k -> q (c k)").bitcast(FP8X4),
+                scales=xh_scales[:].rearrange("q c k -> q (c k)"),
+                in_=live["xh_quads", g][:],
+            )
+            live["xh_codes", g], live["xh_scales", g] = xh_codes, xh_scales
+
+        def gate_matmul(g):
+            for b in range(CHUNKS // CPB):
+                zT = psum.tile([P, CPB, TOK], F32, tag="bank")
+                for i in range(CPB):
+                    m = b * CPB + i
+                    for c in range(2):
+                        nc.tensor.matmul_mx(
+                            out=zT[:, i, :],
+                            lhsT=wu_codes[:, c, m * P : (m + 1) * P].bitcast(FP8X4),
+                            lhsT_scale=wu_scales[:, c, m * P : (m + 1) * P],
+                            rhs=live["xh_codes", g][:, c, :].bitcast(FP8X4),
+                            rhs_scale=live["xh_scales", g][:, c, :],
+                            start=(c == 0),
+                            stop=(c == 1),
+                        )
+                live["zT", g, b] = zT
+
+        def gate_sigmoid(g):
+            uT = early.tile([P, CHUNKS, TOK], F32)
+            for b in range(CHUNKS // CPB):
+                for i in range(CPB):
+                    m = b * CPB + i
+                    nc.scalar.activation(
+                        out=uT[:, m, :], in_=live["zT", g, b][:, i, :], func=ACT.Sigmoid,
+                        bias=column(0, m), scale=1.0,
+                    )
+            live["uT", g] = uT
+
+        def turn_gate_back(g):
+            for t in range(SUB):
+                u_ps = psum.tile([P, H], F32, tag="bank")
+                for m in range(CHUNKS):
+                    nc.tensor.transpose(
+                        u_ps[:, m * P : (m + 1) * P], live["uT", g][:, m, t * P : (t + 1) * P], ident[:]
+                    )
+                live["u", g, t] = u_ps
+
+        def difference(g):
+            diff = early.tile([P, SUB, H], F32, bufs=3)
+            nc.vector.tensor_tensor(out=diff[:], in0=live["s", g][:], in1=live["h", g][:], op=ALU.subtract)
+            live["diff", g] = diff
+
+        def blend(g):
+            gated = early.tile([P, SUB, H], F32)
+            blended = hold.tile([P, SUB, H], F32)
+            sum_p = hold.tile([P, SUB], F32)
+            for t in range(SUB):
+                nc.vector.tensor_tensor(
+                    out=gated[:, t, :].rearrange("p (c f) -> p c f", c=CHUNKS),
+                    in0=live["u", g, t][:].rearrange("p (c f) -> p c f", c=CHUNKS),
+                    in1=live["diff", g][:, t, :].rearrange("p (f c) -> p c f", c=CHUNKS), op=ALU.mult,
+                )
+            for t in range(SUB):
+                nc.vector.scalar_tensor_tensor(
+                    out=blended[:, t, :].rearrange("p (c f) -> p c f", c=CHUNKS),
+                    in0=live["h", g][:, t, :].rearrange("p (f c) -> p c f", c=CHUNKS), scalar=2.0,
+                    in1=gated[:, t, :].rearrange("p (c f) -> p c f", c=CHUNKS),
+                    op0=ALU.mult, op1=ALU.add, accum_out=sum_p[:, t : t + 1],
+                )
+            live["p", g], live["sum_p", g] = blended, sum_p
+
+        def blend_mean(g):
+            neg_mean = hold.tile([P, SUB], F32, name="p_neg_mean")
+            nc.scalar.mul(out=neg_mean[:], in_=live["sum_p", g][:], mul=-1.0 / H)
+            live["p_neg_mean", g] = neg_mean
+
+        def squared_deviations(v, neg_mean, sum_sq, width):
+            for t in range(SUB):
+                squares = early.tile([P, width], BF16)
+                nc.scalar.activation(
+                    out=squares[:], in_=v[:, t, :], func=ACT.Square, bias=neg_mean[:, t : t + 1], scale=1.0,
+                    accum_out=sum_sq[:, t : t + 1],
+                )
+
+        def blend_variance(g):
+            sum_sq = hold.tile([P, SUB], F32, name="p_sum_sq")
+            squared_deviations(live["p", g], live["p_neg_mean", g], sum_sq, H)
+            live["p_sum_sq", g] = sum_sq
+
+        def deviation(sum_sq, width):
+            std = stat.tile([P, SUB], F32)
+            nc.scalar.activation(out=std[:], in_=sum_sq[:], func=ACT.Sqrt, scale=1.0 / width, bias=eps_col[:])
+            return std
+
+        def blend_deviation(g):
+            live["p_std", g] = deviation(live["p_sum_sq", g], H)
+
+        def blend_scale(g):
+            rstd = stat.tile([P, SUB], F32, name="p_rstd")
+            nc.vector.reciprocal(out=rstd[:], in_=live["p_std", g][:])
+            shift = stat.tile([P, SUB], F32, name="p_shift")
+            nc.vector.tensor_tensor(out=shift[:], in0=live["p_neg_mean", g][:], in1=rstd[:], op=ALU.mult)
+            live["p_rstd", g], live["p_shift", g] = rstd, shift
+
+        def normalise(g):
+            normed = late.tile([P, SUB, H], F32)
+            for t in range(SUB):
+                nc.gpsimd.tensor_scalar(
+                    out=normed[:, t, :], in0=live["p", g][:, t, :],
+                    scalar1=live["p_rstd", g][:, t : t + 1], scalar2=live["p_shift", g][:, t : t + 1],
+                    op0=ALU.mult, op1=ALU.add,
+                )
+            live["normed", g] = normed
+
+        def turn_normed(g):
+            for b in range(CHUNKS // CPB):
+                nT = psum.tile([P, CPB, TOK], F32, tag="bank")
+                for i in range(CPB):
+                    m = b * CPB + i
+                    for t in range(SUB):
+                        nc.tensor.transpose(
+                            nT[:, i, t * P : (t + 1) * P], live["normed", g][:, t, m * P : (m + 1) * P], ident[:]
+                        )
+                live["nT", g, b] = nT
+
+        def apply_gain(g):
+            nhT = late.tile([P, CHUNKS, TOK], F32, bufs=4)
+            for b in range(CHUNKS // CPB):
+                for i in range(CPB):
+                    m = b * CPB + i
+                    nc.scalar.activation(
+                        out=nhT[:, m, :], in_=live["nT", g, b][:, i, :], func=ACT.Identity,
+                        scale=column(1, m), bias=column(2, m),
+                    )
+            live["nhT", g] = nhT
+
+        def group_state(g):
+            nh_quads = late.tile([P, TOK, PACK], BF16, align_bytes=64)
+            nc.gpsimd.tensor_scalar(
+                out=nh_quads[:], in0=live["nhT", g][:].rearrange("j m k -> j k m"),
+                scalar1=1.0, scalar2=0.0, op0=ALU.mult, op1=ALU.add,
+            )
+            live["nh_quads", g] = nh_quads
+
+        def quantise_state(g):
+            nh_codes = late.tile([P, TOK], U32, align_bytes=64)
+            nh_scales = late.tile([P, TOK], U8, align_bytes=64)
+            nc.vector.quantize_mx(
+                out=nh_codes[:].bitcast(FP8X4), scales=nh_scales[:],
+                in_=live["nh_quads", g][:].rearrange("j k m -> j (k m)"),
+            )
+            live["nh_codes", g], live["nh_scales", g] = nh_codes, nh_scales
+
+        def turn_state_back(g):
+            for t in range(SUB):
+                nh_ps = psum.tile([P, H], F32, tag="bank")
+                for m in range(CHUNKS):
+                    nc.tensor.transpose(
+                        nh_ps[:, m * P : (m + 1) * P], live["nhT", g][:, m, t * P : (t + 1) * P], ident[:]
+                    )
+                live["nh", g, t] = nh_ps
+
+        def store_state(g):
+            nh_rows = late.tile([P, SUB, H], F32)
+            for t in range(SUB):
+                nc.scalar.copy(
+                    out=nh_rows[:, t, :].rearrange("p (f c) -> p f c", c=CHUNKS),
+                    in_=live["nh", g, t][:].rearrange("p (c f) -> p f c", c=CHUNKS),
+                )
+                nc.sync.dma_start(out=newh_v[:, g * SUB + t, :], in_=nh_rows[:, t, :])
+
+        def output_matmul(g):
+            wd_codes, wd_scales = live["wd"]
+            for t in range(SUB):
+                y_ps = psum.tile([P, D], F32, tag="bank")
+                nc.tensor.matmul_mx(
+                    out=y_ps[:],
+                    lhsT=live["nh_codes", g][:, t * P : (t + 1) * P].bitcast(FP8X4),
+                    lhsT_scale=live["nh_scales", g][:, t * P : (t + 1) * P],
+                    rhs=wd_codes[:, 0, :].bitcast(FP8X4),
+                    rhs_scale=wd_scales[:, 0, :],
+                    start=True,
+                    stop=True,
+                )
+                live["y", g, t] = y_ps
+
+        def add_bias(g):
+            biased = late.tile([P, SUB, D], F32, bufs=3)
+            sum_y = stat.tile([P, SUB], F32)
+            for t in range(SUB):
+                nc.vector.scalar_tensor_tensor(
+                    out=biased[:, t, :], in0=live["y", g, t][:], scalar=1.0, in1=bd_all[:],
+                    op0=ALU.mult, op1=ALU.add, accum_out=sum_y[:, t : t + 1],
+                )
+            live["yb", g], live["sum_y", g] = biased, sum_y
+
+        def output_mean(g):
+            neg_mean = stat.tile([P, SUB], F32, name="y_neg_mean")
+            nc.scalar.mul(out=neg_mean[:], in_=live["sum_y", g][:], mul=-1.0 / D)
+            live["y_neg_mean", g] = neg_mean
+
+        def output_variance(g):
+            sum_sq = stat.tile([P, SUB], F32, name="y_sum_sq")
+            squared_deviations(live["yb", g], live["y_neg_mean", g], sum_sq, D)
+            live["y_sum_sq", g] = sum_sq
+
+        def output_deviation(g):
+            live["y_std", g] = deviation(live["y_sum_sq", g], D)
+
+        def output_scale(g):
+            rstd = stat.tile([P, SUB], F32, name="y_rstd")
+            nc.vector.reciprocal(out=rstd[:], in_=live["y_std", g][:])
+            live["y_rstd", g] = rstd
+
+        def output_gain(g):
+            gained = late.tile([P, SUB, D], F32)
+            for t in range(SUB):
+                nc.vector.scalar_tensor_tensor(
+                    out=gained[:, t, :], in0=live["yb", g][:, t, :], scalar=live["y_neg_mean", g][:, t : t + 1],
+                    in1=live["go_all"][:], op0=ALU.add, op1=ALU.mult,
+                )
+            live["gained", g] = gained
+
+        def output_shift(g):
+            out_rows = late.tile([P, SUB, D], F32)
+            for t in range(SUB):
+                nc.vector.scalar_tensor_tensor(
+                    out=out_rows[:, t, :], in0=live["gained", g][:, t, :], scalar=live["y_rstd", g][:, t : t + 1],
+                    in1=live["bo_all"][:], op0=ALU.mult, op1=ALU.add,
+                )
+                nc.sync.dma_start(out=out_v[:, g * SUB + t, :], in_=out_rows[:, t, :])
+
+        def on(stage, g):
+            if 0 <= g < GROUPS:
+                stage(g)
+
+        for s in range(2 * GROUPS + 5):
+            r = s - (GROUPS + 1)
+            on(load_gate_inputs, s + LOOKAHEAD)
+            on(load_candidate, s + LOOKAHEAD)
+            on(turn_gate_back, s - 2)
+            on(gate_matmul, s - 1)
+            on(turn_inputs, s + 1)
+            on(copy_inputs_out, s)
+            on(difference, s)
+            on(blend, s - 2)
+            on(blend_mean, s - 3)
+            on(blend_variance, s - 3)
+            on(quantise_inputs, s)
+            on(gate_sigmoid, s - 1)
+
+            if r == 1:
+                prepare_second_half()
+            on(blend_deviation, r + 1)
+            on(output_mean, r - 3)
+            on(output_scale, r - 4)
+            on(normalise, r)
+            on(quantise_state, r - 2)
+            on(output_matmul, r - 2)
+            on(apply_gain, r - 1)
+            on(output_shift, r - 4)
+            on(blend_scale, r + 1)
+            on(turn_normed, r)
+            on(group_state, r - 1)
+            on(store_state, r - 4)
+            on(add_bias, r - 2)
+            on(turn_state_back, r - 3)
+            on(output_variance, r - 3)
+            on(output_gain, r - 3)
+            on(output_deviation, r - 3)

@@ -198,7 +198,11 @@ def tile_recurrentffn_pb_t_kernel(
 
         def difference(g):
             diff = early.tile([P, SUB, H], F32, bufs=3)
-            nc.vector.tensor_tensor(out=diff[:], in0=live["s", g][:], in1=live["h", g][:], op=ALU.subtract)
+            nc.vector.tensor_tensor(
+                out=diff[:].rearrange("p t (c f) -> p t c f", c=CHUNKS),
+                in0=live["s", g][:].rearrange("p t (f c) -> p t c f", c=CHUNKS),
+                in1=live["h", g][:].rearrange("p t (f c) -> p t c f", c=CHUNKS), op=ALU.subtract,
+            )
             live["diff", g] = diff
 
         def blend(g):
@@ -207,9 +211,7 @@ def tile_recurrentffn_pb_t_kernel(
             sum_p = hold.tile([P, SUB], F32)
             for t in range(SUB):
                 nc.vector.tensor_tensor(
-                    out=gated[:, t, :].rearrange("p (c f) -> p c f", c=CHUNKS),
-                    in0=live["u", g, t][:].rearrange("p (c f) -> p c f", c=CHUNKS),
-                    in1=live["diff", g][:, t, :].rearrange("p (f c) -> p c f", c=CHUNKS), op=ALU.mult,
+                    out=gated[:, t, :], in0=live["u", g, t][:], in1=live["diff", g][:, t, :], op=ALU.mult
                 )
             for t in range(SUB):
                 nc.vector.scalar_tensor_tensor(

@@ -84,6 +84,8 @@ def tile_recurrentffn_pb_t_kernel(
 
         ident = keep.tile([P, P], F32)
         make_identity(nc, ident[:])
+        twice = keep.tile([P, P], BF16)
+        nc.gpsimd.tensor_scalar(out=twice[:], in0=ident[:], scalar1=2.0, scalar2=0.0, op0=ALU.mult, op1=ALU.add)
         eps_col = keep.tile([P, 1], F32)
         nc.gpsimd.memset(eps_col[:], EPS)
 
@@ -121,15 +123,17 @@ def tile_recurrentffn_pb_t_kernel(
         late = ctx.enter_context(tc.tile_pool(name="late", bufs=2))
 
         wd_raw = late.tile([P, 1, PACK, D], BF16, bufs=1)
-        nc.gpsimd.dma_start(out=wd_raw[:, 0], in_=W_d.rearrange("(p m) n -> p m n", p=P))
         bd_all = keep.tile([P, D], BF16)
-        nc.gpsimd.dma_start(out=bd_all[:], in_=b_d.partition_broadcast(P))
         ones = keep.tile([P, P], BF16)
-        nc.gpsimd.memset(ones[:], 1.0)
         first_rows = late.tile([P, 2, D], BF16, bufs=1)
-        nc.gpsimd.memset(first_rows[:], 0.0)
-        nc.gpsimd.dma_start(out=first_rows[0:1, 0, :], in_=gamma_o.rearrange("(o d) -> o d", o=1))
-        nc.gpsimd.dma_start(out=first_rows[0:1, 1, :], in_=beta_o.rearrange("(o d) -> o d", o=1))
+
+        def load_second_half():
+            nc.gpsimd.memset(ones[:], 1.0)
+            nc.gpsimd.memset(first_rows[:], 0.0)
+            nc.sync.dma_start(out=wd_raw[:, 0], in_=W_d.rearrange("(p m) n -> p m n", p=P))
+            nc.sync.dma_start(out=bd_all[:], in_=b_d.partition_broadcast(P))
+            nc.sync.dma_start(out=first_rows[0:1, 0, :], in_=gamma_o.rearrange("(o d) -> o d", o=1))
+            nc.sync.dma_start(out=first_rows[0:1, 1, :], in_=beta_o.rearrange("(o d) -> o d", o=1))
 
         def prepare_second_half():
             live["wd"] = quantise_weight(nc, late, keep, wd_raw, 1, D, "wd", False)
@@ -196,9 +200,15 @@ def tile_recurrentffn_pb_t_kernel(
                     )
                 live["u", g, t] = u_ps
 
+        def double_state(g):
+            h2 = psum.tile([P, SUB, H], BF16, tag="bank")
+            for t in range(SUB):
+                nc.tensor.matmul(out=h2[:, t, :], lhsT=twice[:], rhs=live["h", g][:, t, :], start=True, stop=True)
+            live["h2", g] = h2
+
         def difference(g):
             diff = early.tile([P, SUB, H], F32, bufs=3)
-            nc.vector.tensor_tensor(
+            nc.gpsimd.tensor_tensor(
                 out=diff[:].rearrange("p t (c f) -> p t c f", c=CHUNKS),
                 in0=live["s", g][:].rearrange("p t (f c) -> p t c f", c=CHUNKS),
                 in1=live["h", g][:].rearrange("p t (f c) -> p t c f", c=CHUNKS), op=ALU.subtract,
@@ -216,7 +226,7 @@ def tile_recurrentffn_pb_t_kernel(
             for t in range(SUB):
                 nc.vector.scalar_tensor_tensor(
                     out=blended[:, t, :].rearrange("p (c f) -> p c f", c=CHUNKS),
-                    in0=live["h", g][:, t, :].rearrange("p (f c) -> p c f", c=CHUNKS), scalar=2.0,
+                    in0=live["h2", g][:, t, :].rearrange("p (f c) -> p c f", c=CHUNKS), scalar=1.0,
                     in1=gated[:, t, :].rearrange("p (c f) -> p c f", c=CHUNKS),
                     op0=ALU.mult, op1=ALU.add, accum_out=sum_p[:, t : t + 1],
                 )
@@ -391,7 +401,10 @@ def tile_recurrentffn_pb_t_kernel(
             r = s - (GROUPS + 1)
             on(load_gate_inputs, s + LOOKAHEAD)
             on(load_candidate, s + LOOKAHEAD)
+            if s == GROUPS // 2:
+                load_second_half()
             on(turn_gate_back, s - 2)
+            on(double_state, s - 2)
             on(gate_matmul, s - 1)
             on(turn_inputs, s + 1)
             on(copy_inputs_out, s)

@@ -21,6 +21,7 @@ TOK = SUB * P
 GROUPS = B // TOK
 BANK = 512
 CPB = BANK // TOK
+SECOND = GROUPS + 1
 LOOKAHEAD = 3
 
 FLOPS = 2 * B * (D + H) * H + 2 * B * H * D
@@ -84,10 +85,10 @@ def tile_recurrentffn_pb_t_kernel(
 
         ident = keep.tile([P, P], F32)
         make_identity(nc, ident[:])
-        twice = keep.tile([P, P], BF16)
-        nc.gpsimd.tensor_scalar(out=twice[:], in0=ident[:], scalar1=2.0, scalar2=0.0, op0=ALU.mult, op1=ALU.add)
         eps_col = keep.tile([P, 1], F32)
         nc.gpsimd.memset(eps_col[:], EPS)
+        twice = keep.tile([P, P], BF16)
+        nc.gpsimd.tensor_scalar(out=twice[:], in0=ident[:], scalar1=2.0, scalar2=0.0, op0=ALU.mult, op1=ALU.add)
 
         def turn_inputs(g):
             for t in range(SUB):
@@ -123,17 +124,15 @@ def tile_recurrentffn_pb_t_kernel(
         late = ctx.enter_context(tc.tile_pool(name="late", bufs=2))
 
         wd_raw = late.tile([P, 1, PACK, D], BF16, bufs=1)
+        nc.gpsimd.dma_start(out=wd_raw[:, 0], in_=W_d.rearrange("(p m) n -> p m n", p=P))
         bd_all = keep.tile([P, D], BF16)
+        nc.gpsimd.dma_start(out=bd_all[:], in_=b_d.partition_broadcast(P))
         ones = keep.tile([P, P], BF16)
+        nc.gpsimd.memset(ones[:], 1.0)
         first_rows = late.tile([P, 2, D], BF16, bufs=1)
-
-        def load_second_half():
-            nc.gpsimd.memset(ones[:], 1.0)
-            nc.gpsimd.memset(first_rows[:], 0.0)
-            nc.sync.dma_start(out=wd_raw[:, 0], in_=W_d.rearrange("(p m) n -> p m n", p=P))
-            nc.sync.dma_start(out=bd_all[:], in_=b_d.partition_broadcast(P))
-            nc.sync.dma_start(out=first_rows[0:1, 0, :], in_=gamma_o.rearrange("(o d) -> o d", o=1))
-            nc.sync.dma_start(out=first_rows[0:1, 1, :], in_=beta_o.rearrange("(o d) -> o d", o=1))
+        nc.gpsimd.memset(first_rows[:], 0.0)
+        nc.gpsimd.dma_start(out=first_rows[0:1, 0, :], in_=gamma_o.rearrange("(o d) -> o d", o=1))
+        nc.gpsimd.dma_start(out=first_rows[0:1, 1, :], in_=beta_o.rearrange("(o d) -> o d", o=1))
 
         def prepare_second_half():
             live["wd"] = quantise_weight(nc, late, keep, wd_raw, 1, D, "wd", False)
@@ -163,8 +162,8 @@ def tile_recurrentffn_pb_t_kernel(
             )
             live["xh_codes", g], live["xh_scales", g] = xh_codes, xh_scales
 
-        def gate_matmul(g):
-            for b in range(CHUNKS // CPB):
+        def gate_matmul(g, banks=range(CHUNKS // CPB)):
+            for b in banks:
                 zT = psum.tile([P, CPB, TOK], F32, tag="bank")
                 for i in range(CPB):
                     m = b * CPB + i
@@ -208,11 +207,12 @@ def tile_recurrentffn_pb_t_kernel(
 
         def difference(g):
             diff = early.tile([P, SUB, H], F32, bufs=3)
-            nc.gpsimd.tensor_tensor(
-                out=diff[:].rearrange("p t (c f) -> p t c f", c=CHUNKS),
-                in0=live["s", g][:].rearrange("p t (f c) -> p t c f", c=CHUNKS),
-                in1=live["h", g][:].rearrange("p t (f c) -> p t c f", c=CHUNKS), op=ALU.subtract,
-            )
+            for t in range(SUB):
+                nc.gpsimd.tensor_tensor(
+                    out=diff[:, t, :].rearrange("p (c f) -> p c f", c=CHUNKS),
+                    in0=live["s", g][:, t, :].rearrange("p (f c) -> p c f", c=CHUNKS),
+                    in1=live["h", g][:, t, :].rearrange("p (f c) -> p c f", c=CHUNKS), op=ALU.subtract,
+                )
             live["diff", g] = diff
 
         def blend(g):
@@ -232,10 +232,15 @@ def tile_recurrentffn_pb_t_kernel(
                 )
             live["p", g], live["sum_p", g] = blended, sum_p
 
+        def negative_mean(pool, total, width, label):
+            neg_mean = pool.tile([P, SUB], F32, name=label)
+            nc.gpsimd.tensor_scalar(
+                out=neg_mean[:], in0=total[:], scalar1=-1.0 / width, scalar2=0.0, op0=ALU.mult, op1=ALU.add
+            )
+            return neg_mean
+
         def blend_mean(g):
-            neg_mean = hold.tile([P, SUB], F32, name="p_neg_mean")
-            nc.scalar.mul(out=neg_mean[:], in_=live["sum_p", g][:], mul=-1.0 / H)
-            live["p_neg_mean", g] = neg_mean
+            live["p_neg_mean", g] = negative_mean(hold, live["sum_p", g], H, "p_neg_mean")
 
         def squared_deviations(v, neg_mean, sum_sq, width):
             for t in range(SUB):
@@ -250,20 +255,20 @@ def tile_recurrentffn_pb_t_kernel(
             squared_deviations(live["p", g], live["p_neg_mean", g], sum_sq, H)
             live["p_sum_sq", g] = sum_sq
 
-        def deviation(sum_sq, width):
-            std = stat.tile([P, SUB], F32)
-            nc.scalar.activation(out=std[:], in_=sum_sq[:], func=ACT.Sqrt, scale=1.0 / width, bias=eps_col[:])
-            return std
-
-        def blend_deviation(g):
-            live["p_std", g] = deviation(live["p_sum_sq", g], H)
+        def inverse_deviation(sum_sq, width, label):
+            rstd = stat.tile([P, SUB], F32, name=label)
+            nc.scalar.activation(
+                out=rstd[:], in_=sum_sq[:], func=ACT.Abs_reciprocal_sqrt, scale=1.0 / width, bias=eps_col[:]
+            )
+            return rstd
 
         def blend_scale(g):
-            rstd = stat.tile([P, SUB], F32, name="p_rstd")
-            nc.vector.reciprocal(out=rstd[:], in_=live["p_std", g][:])
-            shift = stat.tile([P, SUB], F32, name="p_shift")
-            nc.vector.tensor_tensor(out=shift[:], in0=live["p_neg_mean", g][:], in1=rstd[:], op=ALU.mult)
-            live["p_rstd", g], live["p_shift", g] = rstd, shift
+            live["p_rstd", g] = inverse_deviation(live["p_sum_sq", g], H, "p_rstd")
+
+        def blend_shift(g):
+            shift = stat.tile([P, SUB], F32)
+            nc.gpsimd.tensor_tensor(out=shift[:], in0=live["p_neg_mean", g][:], in1=live["p_rstd", g][:], op=ALU.mult)
+            live["p_shift", g] = shift
 
         def normalise(g):
             normed = late.tile([P, SUB, H], F32)
@@ -358,22 +363,15 @@ def tile_recurrentffn_pb_t_kernel(
             live["yb", g], live["sum_y", g] = biased, sum_y
 
         def output_mean(g):
-            neg_mean = stat.tile([P, SUB], F32, name="y_neg_mean")
-            nc.scalar.mul(out=neg_mean[:], in_=live["sum_y", g][:], mul=-1.0 / D)
-            live["y_neg_mean", g] = neg_mean
+            live["y_neg_mean", g] = negative_mean(stat, live["sum_y", g], D, "y_neg_mean")
 
         def output_variance(g):
             sum_sq = stat.tile([P, SUB], F32, name="y_sum_sq")
             squared_deviations(live["yb", g], live["y_neg_mean", g], sum_sq, D)
             live["y_sum_sq", g] = sum_sq
 
-        def output_deviation(g):
-            live["y_std", g] = deviation(live["y_sum_sq", g], D)
-
         def output_scale(g):
-            rstd = stat.tile([P, SUB], F32, name="y_rstd")
-            nc.vector.reciprocal(out=rstd[:], in_=live["y_std", g][:])
-            live["y_rstd", g] = rstd
+            live["y_rstd", g] = inverse_deviation(live["y_sum_sq", g], D, "y_rstd")
 
         def output_gain(g):
             gained = late.tile([P, SUB, D], F32)
@@ -397,12 +395,11 @@ def tile_recurrentffn_pb_t_kernel(
             if 0 <= g < GROUPS:
                 stage(g)
 
-        for s in range(2 * GROUPS + 5):
-            r = s - (GROUPS + 1)
+        for s in range(SECOND + GROUPS + 4):
+            r = s - SECOND
             on(load_gate_inputs, s + LOOKAHEAD)
             on(load_candidate, s + LOOKAHEAD)
-            if s == GROUPS // 2:
-                load_second_half()
+            on(blend_mean, s - 3)
             on(turn_gate_back, s - 2)
             on(double_state, s - 2)
             on(gate_matmul, s - 1)
@@ -410,22 +407,21 @@ def tile_recurrentffn_pb_t_kernel(
             on(copy_inputs_out, s)
             on(difference, s)
             on(blend, s - 2)
-            on(blend_mean, s - 3)
-            on(blend_variance, s - 3)
             on(quantise_inputs, s)
             on(gate_sigmoid, s - 1)
 
             if r == 1:
                 prepare_second_half()
-            on(blend_deviation, r + 1)
-            on(output_mean, r - 3)
+            on(blend_scale, r + 1)
             on(output_scale, r - 4)
             on(normalise, r)
+            on(blend_shift, r + 1)
             on(quantise_state, r - 2)
             on(output_matmul, r - 2)
+            on(output_mean, r - 3)
             on(apply_gain, r - 1)
+            on(blend_variance, s - 3)
             on(output_shift, r - 4)
-            on(blend_scale, r + 1)
             on(turn_normed, r)
             on(group_state, r - 1)
             on(store_state, r - 4)
@@ -433,4 +429,3 @@ def tile_recurrentffn_pb_t_kernel(
             on(turn_state_back, r - 3)
             on(output_variance, r - 3)
             on(output_gain, r - 3)
-            on(output_deviation, r - 3)

@@ -21,30 +21,28 @@ TOK = SUB * P
 GROUPS = B // TOK
 BANK = 512
 CPB = BANK // TOK
-SECOND = GROUPS + 1
+HEAD = 2
+AHEAD = 1
+SECOND = GROUPS + 1 - AHEAD
 LOOKAHEAD = 3
 
 FLOPS = 2 * B * (D + H) * H + 2 * B * H * D
 
 
-def quantise_weight(nc, pool, keep, raw, passes, width, label, deal):
-    quads = pool.tile([P, passes, width, PACK], BF16, align_bytes=64, name=label + "_quads", bufs=1)
-    for c in range(passes):
-        if deal:
-            nc.vector.tensor_copy(
-                out=quads[:, c].rearrange("p (c m) t -> p c m t", c=CHUNKS),
-                in_=raw[:, c].rearrange("p t (m c) -> p c m t", c=CHUNKS),
-            )
-        else:
-            nc.vector.tensor_copy(out=quads[:, c], in_=raw[:, c].rearrange("p t n -> p n t"))
-    codes = keep.tile([P, passes, width], U32, align_bytes=64, name=label + "_codes")
-    scales = keep.tile([P, passes, width], U8, align_bytes=64, name=label + "_scales")
+def lay_quads(engine_copy, quads, raw, cols, deal):
+    if deal:
+        engine_copy(
+            out=quads[:, cols].rearrange("p (c m) t -> p c m t", m=P),
+            in_=raw[:].rearrange("p t (m c) -> p c m t", c=CHUNKS)[:, cols.start // P : cols.stop // P],
+        )
+    else:
+        engine_copy(out=quads[:, cols], in_=raw[:, :, cols].rearrange("p t n -> p n t"))
+
+
+def quantise_pass(nc, quads, codes, scales):
     nc.vector.quantize_mx(
-        out=codes[:].rearrange("p c n -> p (c n)").bitcast(FP8X4),
-        scales=scales[:].rearrange("p c n -> p (c n)"),
-        in_=quads[:].rearrange("p c n t -> p (c n t)"),
+        out=codes.bitcast(FP8X4), scales=scales, in_=quads[:].rearrange("p n t -> p (n t)")
     )
-    return codes, scales
 
 
 def tile_recurrentffn_pb_t_kernel(
@@ -64,7 +62,8 @@ def tile_recurrentffn_pb_t_kernel(
         inp = ctx.enter_context(tc.tile_pool(name="inp", bufs=4))
         early = ctx.enter_context(tc.tile_pool(name="early", bufs=2))
         stat = ctx.enter_context(tc.tile_pool(name="stat", bufs=8))
-        psum = ctx.enter_context(tc.psum_pool(name="psum", bufs=8))
+        const = ctx.enter_context(tc.psum_pool(name="const", bufs=1))
+        psum = ctx.enter_context(tc.psum_pool(name="psum", bufs=7))
 
         live = {}
 
@@ -85,10 +84,15 @@ def tile_recurrentffn_pb_t_kernel(
 
         ident = keep.tile([P, P], F32)
         make_identity(nc, ident[:])
+        power = keep.tile([P, SUB], F32)
+        nc.gpsimd.memset(power[:], -0.5)
         eps_col = keep.tile([P, 1], F32)
         nc.gpsimd.memset(eps_col[:], EPS)
         twice = keep.tile([P, P], BF16)
         nc.gpsimd.tensor_scalar(out=twice[:], in0=ident[:], scalar1=2.0, scalar2=0.0, op0=ALU.mult, op1=ALU.add)
+
+        sigmoid_set = keep.tile([P, 1], F32)
+        nc.scalar.activation(out=sigmoid_set[:], in_=eps_col[:], func=ACT.Sigmoid)
 
         def turn_inputs(g):
             for t in range(SUB):
@@ -99,48 +103,63 @@ def tile_recurrentffn_pb_t_kernel(
                         nc.tensor.transpose(xhT[:, c, u, :], src_words[:, u : 2 * P : 2], ident[:])
                 live["xhT", g, t] = xhT
 
-        with tc.tile_pool(name="prep", bufs=1) as prep:
-            load_gate_inputs(0)
-            wu_raw = prep.tile([P, 2, PACK, H], BF16)
-            wu_v = W_u.rearrange("(c p t) n -> c p t n", c=2, p=P)
-            for c in range(2):
-                nc.sync.dma_start(out=wu_raw[:, c], in_=wu_v[c])
-            load_candidate(0)
-            for g in range(1, LOOKAHEAD):
-                load_gate_inputs(g)
-                load_candidate(g)
-            turn_inputs(0)
+        prep = ctx.enter_context(tc.tile_pool(name="prep", bufs=1))
+        late = ctx.enter_context(tc.tile_pool(name="late", bufs=2))
+        load_gate_inputs(0)
+        wu_v = W_u.rearrange("(c p t) n -> c p t n", c=2, p=P)
+        wu_raw = []
+        for c in range(2):
+            raw = prep.tile([P, PACK, H], BF16, name="wu_raw%d" % c)
+            nc.sync.dma_start(out=raw[:], in_=wu_v[c])
+            wu_raw.append(raw)
+        load_candidate(0)
+        for g in range(1, LOOKAHEAD):
+            load_gate_inputs(g)
+            load_candidate(g)
+        turn_inputs(0)
 
-            vec_raw = prep.tile([P, 3, 16], BF16)
-            for v, vec in enumerate((b_u, gamma_h, beta_h)):
-                nc.gpsimd.dma_start(out=vec_raw[:, v, :CHUNKS], in_=vec.rearrange("(p c) -> p c", c=CHUNKS))
-            vec_cols = keep.tile([P, 3, CHUNKS], F32)
-            nc.gpsimd.tensor_copy(out=vec_cols[:], in_=vec_raw[:, :, :CHUNKS])
-            wu_codes, wu_scales = quantise_weight(nc, prep, keep, wu_raw, 2, H, "wu", True)
+        vec_raw = keep.tile([P, 3, 16], BF16)
+        for v, vec in enumerate((b_u, gamma_h, beta_h)):
+            nc.gpsimd.dma_start(out=vec_raw[:, v, :CHUNKS], in_=vec.rearrange("(p c) -> p c", c=CHUNKS))
+        wu_codes = keep.tile([P, 2, H], U32, align_bytes=64)
+        wu_scales = keep.tile([P, 2, H], U8, align_bytes=64)
+        wu_quads = []
+        for c in range(2):
+            quads = prep.tile([P, H, PACK], BF16, align_bytes=64, name="wu_quads%d" % c)
+            wu_quads.append(quads)
+        lay_quads(nc.vector.tensor_copy, wu_quads[0], wu_raw[0], slice(0, H), True)
+        lay_quads(nc.vector.tensor_copy, wu_quads[1], wu_raw[1], slice(0, H // 2), True)
+        quantise_pass(nc, wu_quads[0], wu_codes[:, 0], wu_scales[:, 0])
 
         def column(v, m):
-            return vec_cols[:, v, m : m + 1]
+            return vec_cols[:, v - 1, m : m + 1]
 
-        late = ctx.enter_context(tc.tile_pool(name="late", bufs=2))
-
-        wd_raw = late.tile([P, 1, PACK, D], BF16, bufs=1)
-        nc.gpsimd.dma_start(out=wd_raw[:, 0], in_=W_d.rearrange("(p m) n -> p m n", p=P))
+        vec_cols = keep.tile([P, 2, CHUNKS], F32)
+        wd_raw = late.tile([P, PACK, D], BF16, bufs=1)
         bd_all = keep.tile([P, D], BF16)
-        nc.gpsimd.dma_start(out=bd_all[:], in_=b_d.partition_broadcast(P))
         ones = keep.tile([P, P], BF16)
-        nc.gpsimd.memset(ones[:], 1.0)
         first_rows = late.tile([P, 2, D], BF16, bufs=1)
-        nc.gpsimd.memset(first_rows[:], 0.0)
-        nc.gpsimd.dma_start(out=first_rows[0:1, 0, :], in_=gamma_o.rearrange("(o d) -> o d", o=1))
-        nc.gpsimd.dma_start(out=first_rows[0:1, 1, :], in_=beta_o.rearrange("(o d) -> o d", o=1))
+
+        def load_second_half():
+            nc.gpsimd.tensor_copy(out=vec_cols[:], in_=vec_raw[:, 1:, :CHUNKS])
+            nc.gpsimd.memset(ones[:], 1.0)
+            nc.gpsimd.memset(first_rows[:], 0.0)
+            nc.sync.dma_start(out=wd_raw[:], in_=W_d.rearrange("(p t) n -> p t n", p=P))
+            nc.sync.dma_start(out=bd_all[:], in_=b_d.partition_broadcast(P))
+            nc.sync.dma_start(out=first_rows[0:1, 0, :], in_=gamma_o.rearrange("(o d) -> o d", o=1))
+            nc.sync.dma_start(out=first_rows[0:1, 1, :], in_=beta_o.rearrange("(o d) -> o d", o=1))
 
         def prepare_second_half():
-            live["wd"] = quantise_weight(nc, late, keep, wd_raw, 1, D, "wd", False)
-            go_all = psum.tile([P, D], F32, tag="bank")
-            nc.tensor.matmul(out=go_all[:], lhsT=ones[:], rhs=first_rows[:, 0, :], start=True, stop=True)
-            bo_all = psum.tile([P, D], F32, tag="bank")
-            nc.tensor.matmul(out=bo_all[:], lhsT=ones[:], rhs=first_rows[:, 1, :], start=True, stop=True)
-            live["go_all"], live["bo_all"] = go_all, bo_all
+            wd_quads = late.tile([P, D, PACK], BF16, align_bytes=64, bufs=1)
+            wd_codes = keep.tile([P, D], U32, align_bytes=64)
+            wd_scales = keep.tile([P, D], U8, align_bytes=64)
+            lay_quads(nc.vector.tensor_copy, wd_quads, wd_raw, slice(0, D), False)
+            quantise_pass(nc, wd_quads, wd_codes[:], wd_scales[:])
+            gain_shift = const.tile([P, 2, D], BF16)
+            for v in range(2):
+                nc.tensor.matmul(out=gain_shift[:, v, :], lhsT=ones[:], rhs=first_rows[:, v, :], start=True, stop=True)
+            live["wd"] = wd_codes, wd_scales
+            live["go_all"], live["bo_all"] = gain_shift[:, 0, :], gain_shift[:, 1, :]
 
         def copy_inputs_out(g):
             xh_quads = early.tile([P, 2 * TOK * PACK], BF16, align_bytes=64)
@@ -186,7 +205,7 @@ def tile_recurrentffn_pb_t_kernel(
                     m = b * CPB + i
                     nc.scalar.activation(
                         out=uT[:, m, :], in_=live["zT", g, b][:, i, :], func=ACT.Sigmoid,
-                        bias=column(0, m), scale=1.0,
+                        bias=vec_raw[:, 0, m : m + 1], scale=1.0,
                     )
             live["uT", g] = uT
 
@@ -207,8 +226,9 @@ def tile_recurrentffn_pb_t_kernel(
 
         def difference(g):
             diff = early.tile([P, SUB, H], F32, bufs=3)
+            engine = nc.vector if g < HEAD else nc.gpsimd
             for t in range(SUB):
-                nc.gpsimd.tensor_tensor(
+                engine.tensor_tensor(
                     out=diff[:, t, :].rearrange("p (c f) -> p c f", c=CHUNKS),
                     in0=live["s", g][:, t, :].rearrange("p (f c) -> p c f", c=CHUNKS),
                     in1=live["h", g][:, t, :].rearrange("p (f c) -> p c f", c=CHUNKS), op=ALU.subtract,
@@ -263,7 +283,17 @@ def tile_recurrentffn_pb_t_kernel(
             return rstd
 
         def blend_scale(g):
-            live["p_rstd", g] = inverse_deviation(live["p_sum_sq", g], H, "p_rstd")
+            if g >= AHEAD:
+                live["p_rstd", g] = inverse_deviation(live["p_sum_sq", g], H, "p_rstd")
+
+        def blend_power(g):
+            var = stat.tile([P, SUB], F32)
+            nc.gpsimd.tensor_scalar(
+                out=var[:], in0=live["p_sum_sq", g][:], scalar1=1.0 / H, scalar2=EPS, op0=ALU.mult, op1=ALU.add
+            )
+            rstd = keep.tile([P, SUB], F32, name="p_rstd%d" % g)
+            nc.gpsimd.tensor_tensor(out=rstd[:], in0=var[:], in1=power[:], op=ALU.pow)
+            live["p_rstd", g] = rstd
 
         def blend_shift(g):
             shift = stat.tile([P, SUB], F32)
@@ -345,8 +375,8 @@ def tile_recurrentffn_pb_t_kernel(
                     out=y_ps[:],
                     lhsT=live["nh_codes", g][:, t * P : (t + 1) * P].bitcast(FP8X4),
                     lhsT_scale=live["nh_scales", g][:, t * P : (t + 1) * P],
-                    rhs=wd_codes[:, 0, :].bitcast(FP8X4),
-                    rhs_scale=wd_scales[:, 0, :],
+                    rhs=wd_codes[:].bitcast(FP8X4),
+                    rhs_scale=wd_scales[:],
                     start=True,
                     stop=True,
                 )
@@ -378,7 +408,7 @@ def tile_recurrentffn_pb_t_kernel(
             for t in range(SUB):
                 nc.vector.scalar_tensor_tensor(
                     out=gained[:, t, :], in0=live["yb", g][:, t, :], scalar=live["y_neg_mean", g][:, t : t + 1],
-                    in1=live["go_all"][:], op0=ALU.add, op1=ALU.mult,
+                    in1=live["go_all"], op0=ALU.add, op1=ALU.mult,
                 )
             live["gained", g] = gained
 
@@ -387,7 +417,7 @@ def tile_recurrentffn_pb_t_kernel(
             for t in range(SUB):
                 nc.vector.scalar_tensor_tensor(
                     out=out_rows[:, t, :], in0=live["gained", g][:, t, :], scalar=live["y_rstd", g][:, t : t + 1],
-                    in1=live["bo_all"][:], op0=ALU.mult, op1=ALU.add,
+                    in1=live["bo_all"], op0=ALU.mult, op1=ALU.add,
                 )
                 nc.sync.dma_start(out=out_v[:, g * SUB + t, :], in_=out_rows[:, t, :])
 
@@ -397,20 +427,28 @@ def tile_recurrentffn_pb_t_kernel(
 
         for s in range(SECOND + GROUPS + 4):
             r = s - SECOND
+            if s == GROUPS // 2:
+                load_second_half()
             on(load_gate_inputs, s + LOOKAHEAD)
             on(load_candidate, s + LOOKAHEAD)
             on(blend_mean, s - 3)
+            if s - 4 < AHEAD:
+                on(blend_power, s - 4)
             on(turn_gate_back, s - 2)
             on(double_state, s - 2)
             on(gate_matmul, s - 1)
             on(turn_inputs, s + 1)
             on(copy_inputs_out, s)
+            if s == 0:
+                lay_quads(nc.scalar.copy, wu_quads[1], wu_raw[1], slice(H // 2, H), True)
             on(difference, s)
             on(blend, s - 2)
             on(quantise_inputs, s)
+            if s == 0:
+                quantise_pass(nc, wu_quads[1], wu_codes[:, 1], wu_scales[:, 1])
             on(gate_sigmoid, s - 1)
 
-            if r == 1:
+            if r == 0:
                 prepare_second_half()
             on(blend_scale, r + 1)
             on(output_scale, r - 4)

@@ -21,6 +21,7 @@ TOK = SUB * P
 GROUPS = B // TOK
 BANK = 512
 CPB = BANK // TOK
+LINE = 4
 HEAD = 2
 AHEAD = 1
 SECOND = GROUPS + 1 - AHEAD
@@ -229,9 +230,9 @@ def tile_recurrentffn_pb_t_kernel(
             engine = nc.vector if g < HEAD else nc.gpsimd
             for t in range(SUB):
                 engine.tensor_tensor(
-                    out=diff[:, t, :].rearrange("p (c f) -> p c f", c=CHUNKS),
-                    in0=live["s", g][:, t, :].rearrange("p (f c) -> p c f", c=CHUNKS),
-                    in1=live["h", g][:, t, :].rearrange("p (f c) -> p c f", c=CHUNKS), op=ALU.subtract,
+                    out=diff[:, t, :].rearrange("p (c f i) -> p f c i", c=CHUNKS, i=LINE),
+                    in0=live["s", g][:, t, :].rearrange("p (f i c) -> p f c i", c=CHUNKS, i=LINE),
+                    in1=live["h", g][:, t, :].rearrange("p (f i c) -> p f c i", c=CHUNKS, i=LINE), op=ALU.subtract,
                 )
             live["diff", g] = diff
 
@@ -335,7 +336,8 @@ def tile_recurrentffn_pb_t_kernel(
         def group_state(g):
             nh_quads = late.tile([P, TOK, PACK], BF16, align_bytes=64)
             nc.gpsimd.tensor_scalar(
-                out=nh_quads[:], in0=live["nhT", g][:].rearrange("j m k -> j k m"),
+                out=nh_quads[:].rearrange("j (k i) m -> j k m i", i=LINE),
+                in0=live["nhT", g][:].rearrange("j m (k i) -> j k m i", i=LINE),
                 scalar1=1.0, scalar2=0.0, op0=ALU.mult, op1=ALU.add,
             )
             live["nh_quads", g] = nh_quads

@@ -85,8 +85,13 @@ def tile_recurrentffn_pb_t_kernel(
 
         ident = keep.tile([P, P], F32)
         make_identity(nc, ident[:])
-        power = keep.tile([P, SUB], F32)
+        power = keep.tile([P, AHEAD, SUB], F32)
         nc.gpsimd.memset(power[:], -0.5)
+        p_sum = keep.tile([P, GROUPS, SUB], F32)
+        p_squares = keep.tile([P, GROUPS, SUB], F32)
+        p_mean = keep.tile([P, GROUPS, SUB], F32)
+        p_rstd = keep.tile([P, GROUPS, SUB], F32)
+        p_var = keep.tile([P, AHEAD, SUB], F32)
         eps_col = keep.tile([P, 1], F32)
         nc.gpsimd.memset(eps_col[:], EPS)
         twice = keep.tile([P, P], BF16)
@@ -239,7 +244,6 @@ def tile_recurrentffn_pb_t_kernel(
         def blend(g):
             gated = early.tile([P, SUB, H], F32)
             blended = hold.tile([P, SUB, H], F32)
-            sum_p = hold.tile([P, SUB], F32)
             for t in range(SUB):
                 nc.vector.tensor_tensor(
                     out=gated[:, t, :], in0=live["u", g, t][:], in1=live["diff", g][:, t, :], op=ALU.mult
@@ -249,65 +253,49 @@ def tile_recurrentffn_pb_t_kernel(
                     out=blended[:, t, :].rearrange("p (c f) -> p c f", c=CHUNKS),
                     in0=live["h2", g][:, t, :].rearrange("p (f c) -> p c f", c=CHUNKS), scalar=1.0,
                     in1=gated[:, t, :].rearrange("p (c f) -> p c f", c=CHUNKS),
-                    op0=ALU.mult, op1=ALU.add, accum_out=sum_p[:, t : t + 1],
+                    op0=ALU.mult, op1=ALU.add, accum_out=p_sum[:, g, t : t + 1],
                 )
-            live["p", g], live["sum_p", g] = blended, sum_p
+            live["p", g] = blended
 
-        def negative_mean(pool, total, width, label):
-            neg_mean = pool.tile([P, SUB], F32, name=label)
-            nc.gpsimd.tensor_scalar(
-                out=neg_mean[:], in0=total[:], scalar1=-1.0 / width, scalar2=0.0, op0=ALU.mult, op1=ALU.add
-            )
-            return neg_mean
-
-        def blend_mean(g):
-            live["p_neg_mean", g] = negative_mean(hold, live["sum_p", g], H, "p_neg_mean")
-
-        def squared_deviations(v, neg_mean, sum_sq, width):
+        def squared_deviations(v, total, squares, width):
             for t in range(SUB):
-                squares = early.tile([P, width], BF16)
+                junk = early.tile([P, width], BF16)
                 nc.scalar.activation(
-                    out=squares[:], in_=v[:, t, :], func=ACT.Square, bias=neg_mean[:, t : t + 1], scale=1.0,
-                    accum_out=sum_sq[:, t : t + 1],
+                    out=junk[:], in_=v[:, t, :], func=ACT.Square, bias=total[:, t : t + 1], scale=-float(width),
+                    accum_out=squares[:, t : t + 1],
                 )
 
         def blend_variance(g):
-            sum_sq = hold.tile([P, SUB], F32, name="p_sum_sq")
-            squared_deviations(live["p", g], live["p_neg_mean", g], sum_sq, H)
-            live["p_sum_sq", g] = sum_sq
+            squared_deviations(live["p", g], p_sum[:, g], p_squares[:, g], H)
 
-        def inverse_deviation(sum_sq, width, label):
-            rstd = stat.tile([P, SUB], F32, name=label)
-            nc.scalar.activation(
-                out=rstd[:], in_=sum_sq[:], func=ACT.Abs_reciprocal_sqrt, scale=1.0 / width, bias=eps_col[:]
-            )
-            return rstd
+        def mean(out, total, width):
+            nc.gpsimd.tensor_scalar(out=out, in0=total, scalar1=1.0 / width, scalar2=0.0, op0=ALU.mult, op1=ALU.add)
 
-        def blend_scale(g):
-            if g >= AHEAD:
-                live["p_rstd", g] = inverse_deviation(live["p_sum_sq", g], H, "p_rstd")
-
-        def blend_power(g):
-            var = stat.tile([P, SUB], F32)
+        def blend_powers():
+            groups = slice(0, AHEAD)
+            mean(p_mean[:, groups], p_sum[:, groups], H)
             nc.gpsimd.tensor_scalar(
-                out=var[:], in0=live["p_sum_sq", g][:], scalar1=1.0 / H, scalar2=EPS, op0=ALU.mult, op1=ALU.add
+                out=p_var[:], in0=p_squares[:, groups], scalar1=1.0 / H**3, scalar2=EPS, op0=ALU.mult, op1=ALU.add
             )
-            rstd = keep.tile([P, SUB], F32, name="p_rstd%d" % g)
-            nc.gpsimd.tensor_tensor(out=rstd[:], in0=var[:], in1=power[:], op=ALU.pow)
-            live["p_rstd", g] = rstd
+            nc.gpsimd.tensor_tensor(out=p_rstd[:, groups], in0=p_var[:], in1=power[:], op=ALU.pow)
 
-        def blend_shift(g):
-            shift = stat.tile([P, SUB], F32)
-            nc.gpsimd.tensor_tensor(out=shift[:], in0=live["p_neg_mean", g][:], in1=live["p_rstd", g][:], op=ALU.mult)
-            live["p_shift", g] = shift
+        def inverse_deviation(out, squares, width):
+            nc.scalar.activation(
+                out=out, in_=squares, func=ACT.Abs_reciprocal_sqrt, scale=1.0 / width**3, bias=eps_col[:]
+            )
+
+        def blend_scales(first, end):
+            groups = slice(first, end)
+            inverse_deviation(p_rstd[:, groups], p_squares[:, groups], H)
+            mean(p_mean[:, groups], p_sum[:, groups], H)
 
         def normalise(g):
             normed = late.tile([P, SUB, H], F32)
             for t in range(SUB):
                 nc.gpsimd.tensor_scalar(
                     out=normed[:, t, :], in0=live["p", g][:, t, :],
-                    scalar1=live["p_rstd", g][:, t : t + 1], scalar2=live["p_shift", g][:, t : t + 1],
-                    op0=ALU.mult, op1=ALU.add,
+                    scalar1=p_mean[:, g, t : t + 1], scalar2=p_rstd[:, g, t : t + 1],
+                    op0=ALU.subtract, op1=ALU.mult,
                 )
             live["normed", g] = normed
 
@@ -395,22 +383,26 @@ def tile_recurrentffn_pb_t_kernel(
             live["yb", g], live["sum_y", g] = biased, sum_y
 
         def output_mean(g):
-            live["y_neg_mean", g] = negative_mean(stat, live["sum_y", g], D, "y_neg_mean")
+            y_mean = stat.tile([P, SUB], F32)
+            mean(y_mean[:], live["sum_y", g][:], D)
+            live["y_mean", g] = y_mean
 
         def output_variance(g):
-            sum_sq = stat.tile([P, SUB], F32, name="y_sum_sq")
-            squared_deviations(live["yb", g], live["y_neg_mean", g], sum_sq, D)
-            live["y_sum_sq", g] = sum_sq
+            y_squares = stat.tile([P, SUB], F32)
+            squared_deviations(live["yb", g], live["sum_y", g], y_squares, D)
+            live["y_squares", g] = y_squares
 
         def output_scale(g):
-            live["y_rstd", g] = inverse_deviation(live["y_sum_sq", g], D, "y_rstd")
+            y_rstd = stat.tile([P, SUB], F32)
+            inverse_deviation(y_rstd[:], live["y_squares", g][:], D)
+            live["y_rstd", g] = y_rstd
 
         def output_gain(g):
             gained = late.tile([P, SUB, D], F32)
             for t in range(SUB):
                 nc.vector.scalar_tensor_tensor(
-                    out=gained[:, t, :], in0=live["yb", g][:, t, :], scalar=live["y_neg_mean", g][:, t : t + 1],
-                    in1=live["go_all"], op0=ALU.add, op1=ALU.mult,
+                    out=gained[:, t, :], in0=live["yb", g][:, t, :], scalar=live["y_mean", g][:, t : t + 1],
+                    in1=live["go_all"], op0=ALU.subtract, op1=ALU.mult,
                 )
             live["gained", g] = gained
 
@@ -433,9 +425,8 @@ def tile_recurrentffn_pb_t_kernel(
                 load_second_half()
             on(load_gate_inputs, s + LOOKAHEAD)
             on(load_candidate, s + LOOKAHEAD)
-            on(blend_mean, s - 3)
-            if s - 4 < AHEAD:
-                on(blend_power, s - 4)
+            if s == AHEAD + 3:
+                blend_powers()
             on(turn_gate_back, s - 2)
             on(double_state, s - 2)
             on(gate_matmul, s - 1)
@@ -452,10 +443,12 @@ def tile_recurrentffn_pb_t_kernel(
 
             if r == 0:
                 prepare_second_half()
-            on(blend_scale, r + 1)
+            if s == GROUPS:
+                blend_scales(AHEAD, GROUPS - 3)
+            if s == GROUPS + 3:
+                blend_scales(GROUPS - 3, GROUPS)
             on(output_scale, r - 4)
             on(normalise, r)
-            on(blend_shift, r + 1)
             on(quantise_state, r - 2)
             on(output_matmul, r - 2)
             on(output_mean, r - 3)
@@ -464,8 +457,8 @@ def tile_recurrentffn_pb_t_kernel(
             on(output_shift, r - 4)
             on(turn_normed, r)
             on(group_state, r - 1)
-            on(store_state, r - 4)
+            on(store_state, r - 3)
             on(add_bias, r - 2)
-            on(turn_state_back, r - 3)
+            on(turn_state_back, r - 2)
             on(output_variance, r - 3)
             on(output_gain, r - 3)

@@ -89,8 +89,9 @@ def tile_recurrentffn_pb_t_kernel(
         nc.gpsimd.memset(power[:], -0.5)
         p_sum = keep.tile([P, GROUPS, SUB], F32)
         p_squares = keep.tile([P, GROUPS, SUB], F32)
-        p_mean = keep.tile([P, GROUPS, SUB], F32)
+        p_neg_mean = keep.tile([P, GROUPS, SUB], F32)
         p_rstd = keep.tile([P, GROUPS, SUB], F32)
+        p_shift = keep.tile([P, GROUPS, SUB], F32)
         p_var = keep.tile([P, AHEAD, SUB], F32)
         eps_col = keep.tile([P, 1], F32)
         nc.gpsimd.memset(eps_col[:], EPS)
@@ -268,16 +269,25 @@ def tile_recurrentffn_pb_t_kernel(
         def blend_variance(g):
             squared_deviations(live["p", g], p_sum[:, g], p_squares[:, g], H)
 
-        def mean(out, total, width):
-            nc.gpsimd.tensor_scalar(out=out, in0=total, scalar1=1.0 / width, scalar2=0.0, op0=ALU.mult, op1=ALU.add)
+        def negative_mean(out, total, width):
+            nc.gpsimd.tensor_scalar(out=out, in0=total, scalar1=-1.0 / width, scalar2=0.0, op0=ALU.mult, op1=ALU.add)
+
+        def blend_means(first, end):
+            negative_mean(p_neg_mean[:, first:end], p_sum[:, first:end], H)
+
+        def blend_shifts(first, end):
+            groups = slice(first, end)
+            nc.gpsimd.tensor_tensor(
+                out=p_shift[:, groups], in0=p_neg_mean[:, groups], in1=p_rstd[:, groups], op=ALU.mult
+            )
 
         def blend_powers():
             groups = slice(0, AHEAD)
-            mean(p_mean[:, groups], p_sum[:, groups], H)
             nc.gpsimd.tensor_scalar(
                 out=p_var[:], in0=p_squares[:, groups], scalar1=1.0 / H**3, scalar2=EPS, op0=ALU.mult, op1=ALU.add
             )
             nc.gpsimd.tensor_tensor(out=p_rstd[:, groups], in0=p_var[:], in1=power[:], op=ALU.pow)
+            blend_shifts(0, AHEAD)
 
         def inverse_deviation(out, squares, width):
             nc.scalar.activation(
@@ -285,17 +295,15 @@ def tile_recurrentffn_pb_t_kernel(
             )
 
         def blend_scales(first, end):
-            groups = slice(first, end)
-            inverse_deviation(p_rstd[:, groups], p_squares[:, groups], H)
-            mean(p_mean[:, groups], p_sum[:, groups], H)
+            inverse_deviation(p_rstd[:, first:end], p_squares[:, first:end], H)
 
         def normalise(g):
             normed = late.tile([P, SUB, H], F32)
             for t in range(SUB):
                 nc.gpsimd.tensor_scalar(
                     out=normed[:, t, :], in0=live["p", g][:, t, :],
-                    scalar1=p_mean[:, g, t : t + 1], scalar2=p_rstd[:, g, t : t + 1],
-                    op0=ALU.subtract, op1=ALU.mult,
+                    scalar1=p_rstd[:, g, t : t + 1], scalar2=p_shift[:, g, t : t + 1],
+                    op0=ALU.mult, op1=ALU.add,
                 )
             live["normed", g] = normed
 
@@ -322,7 +330,7 @@ def tile_recurrentffn_pb_t_kernel(
             live["nhT", g] = nhT
 
         def group_state(g):
-            nh_quads = late.tile([P, TOK, PACK], BF16, align_bytes=64)
+            nh_quads = late.tile([P, TOK, PACK], BF16, align_bytes=64, bufs=1)
             nc.gpsimd.tensor_scalar(
                 out=nh_quads[:].rearrange("j (k i) m -> j k m i", i=LINE),
                 in0=live["nhT", g][:].rearrange("j m (k i) -> j k m i", i=LINE),
@@ -383,9 +391,9 @@ def tile_recurrentffn_pb_t_kernel(
             live["yb", g], live["sum_y", g] = biased, sum_y
 
         def output_mean(g):
-            y_mean = stat.tile([P, SUB], F32)
-            mean(y_mean[:], live["sum_y", g][:], D)
-            live["y_mean", g] = y_mean
+            y_neg_mean = stat.tile([P, SUB], F32)
+            negative_mean(y_neg_mean[:], live["sum_y", g][:], D)
+            live["y_neg_mean", g] = y_neg_mean
 
         def output_variance(g):
             y_squares = stat.tile([P, SUB], F32)
@@ -401,8 +409,8 @@ def tile_recurrentffn_pb_t_kernel(
             gained = late.tile([P, SUB, D], F32)
             for t in range(SUB):
                 nc.vector.scalar_tensor_tensor(
-                    out=gained[:, t, :], in0=live["yb", g][:, t, :], scalar=live["y_mean", g][:, t : t + 1],
-                    in1=live["go_all"], op0=ALU.subtract, op1=ALU.mult,
+                    out=gained[:, t, :], in0=live["yb", g][:, t, :], scalar=live["y_neg_mean", g][:, t : t + 1],
+                    in1=live["go_all"], op0=ALU.add, op1=ALU.mult,
                 )
             live["gained", g] = gained
 
@@ -426,7 +434,12 @@ def tile_recurrentffn_pb_t_kernel(
             on(load_gate_inputs, s + LOOKAHEAD)
             on(load_candidate, s + LOOKAHEAD)
             if s == AHEAD + 3:
+                blend_means(0, AHEAD)
                 blend_powers()
+            if s == GROUPS:
+                blend_means(AHEAD, GROUPS - 3)
+            if s == GROUPS + 3:
+                blend_means(GROUPS - 3, GROUPS)
             on(turn_gate_back, s - 2)
             on(double_state, s - 2)
             on(gate_matmul, s - 1)
@@ -449,6 +462,10 @@ def tile_recurrentffn_pb_t_kernel(
                 blend_scales(GROUPS - 3, GROUPS)
             on(output_scale, r - 4)
             on(normalise, r)
+            if s == GROUPS:
+                blend_shifts(AHEAD, GROUPS - 3)
+            if s == GROUPS + 3:
+                blend_shifts(GROUPS - 3, GROUPS)
             on(quantise_state, r - 2)
             on(output_matmul, r - 2)
             on(output_mean, r - 3)

@@ -22,9 +22,9 @@ GROUPS = B // TOK
 BANK = 512
 CPB = BANK // TOK
 LINE = 4
-HEAD = 2
-AHEAD = 1
-SECOND = GROUPS + 1 - AHEAD
+HEAD = 3
+AHEAD = 2
+SECOND = GROUPS
 LOOKAHEAD = 3
 
 FLOPS = 2 * B * (D + H) * H + 2 * B * H * D
@@ -123,6 +123,8 @@ def tile_recurrentffn_pb_t_kernel(
         for g in range(1, LOOKAHEAD):
             load_gate_inputs(g)
             load_candidate(g)
+        wd_raw = prep.tile([P, PACK, D], BF16)
+        nc.sync.dma_start(out=wd_raw[:], in_=W_d.rearrange("(p t) n -> p t n", p=P))
         turn_inputs(0)
 
         vec_raw = keep.tile([P, 3, 16], BF16)
@@ -142,7 +144,7 @@ def tile_recurrentffn_pb_t_kernel(
             return vec_cols[:, v - 1, m : m + 1]
 
         vec_cols = keep.tile([P, 2, CHUNKS], F32)
-        wd_raw = late.tile([P, PACK, D], BF16, bufs=1)
+        wd_quads = late.tile([P, D, PACK], BF16, align_bytes=64, bufs=1)
         bd_all = keep.tile([P, D], BF16)
         ones = keep.tile([P, P], BF16)
         first_rows = late.tile([P, 2, D], BF16, bufs=1)
@@ -151,16 +153,13 @@ def tile_recurrentffn_pb_t_kernel(
             nc.gpsimd.tensor_copy(out=vec_cols[:], in_=vec_raw[:, 1:, :CHUNKS])
             nc.gpsimd.memset(ones[:], 1.0)
             nc.gpsimd.memset(first_rows[:], 0.0)
-            nc.sync.dma_start(out=wd_raw[:], in_=W_d.rearrange("(p t) n -> p t n", p=P))
             nc.sync.dma_start(out=bd_all[:], in_=b_d.partition_broadcast(P))
             nc.sync.dma_start(out=first_rows[0:1, 0, :], in_=gamma_o.rearrange("(o d) -> o d", o=1))
             nc.sync.dma_start(out=first_rows[0:1, 1, :], in_=beta_o.rearrange("(o d) -> o d", o=1))
 
         def prepare_second_half():
-            wd_quads = late.tile([P, D, PACK], BF16, align_bytes=64, bufs=1)
             wd_codes = keep.tile([P, D], U32, align_bytes=64)
             wd_scales = keep.tile([P, D], U8, align_bytes=64)
-            lay_quads(nc.vector.tensor_copy, wd_quads, wd_raw, slice(0, D), False)
             quantise_pass(nc, wd_quads, wd_codes[:], wd_scales[:])
             gain_shift = const.tile([P, 2, D], BF16)
             for v in range(2):
@@ -452,6 +451,8 @@ def tile_recurrentffn_pb_t_kernel(
             on(quantise_inputs, s)
             if s == 0:
                 quantise_pass(nc, wu_quads[1], wu_codes[:, 1], wu_scales[:, 1])
+            if s == 1:
+                lay_quads(nc.vector.tensor_copy, wd_quads, wd_raw, slice(0, D), False)
             on(gate_sigmoid, s - 1)
 
             if r == 0:

from contextlib import ExitStack

import concourse.mybir as mybir
from concourse.masks import make_identity

F32 = mybir.dt.float32
BF16 = mybir.dt.bfloat16
U32 = mybir.dt.uint32
U8 = mybir.dt.uint8
FP8X4 = mybir.dt.float8_e4m3fn_x4
ALU = mybir.AluOpType
ACT = mybir.ActivationFunctionType

P = 128
PACK = 4
B, D, H = 4096, 512, 512
EPS = 1e-3
CHUNKS = H // P
SUB = 2
TOK = SUB * P
GROUPS = B // TOK
BANK = 512
CPB = BANK // TOK
LINE = 4
HEAD = 3
AHEAD = 2
SECOND = GROUPS
LOOKAHEAD = 3

FLOPS = 2 * B * (D + H) * H + 2 * B * H * D


def lay_quads(engine_copy, quads, raw, cols, deal):
    if deal:
        engine_copy(
            out=quads[:, cols].rearrange("p (c m) t -> p c m t", m=P),
            in_=raw[:].rearrange("p t (m c) -> p c m t", c=CHUNKS)[:, cols.start // P : cols.stop // P],
        )
    else:
        engine_copy(out=quads[:, cols], in_=raw[:, :, cols].rearrange("p t n -> p n t"))


def quantise_pass(nc, quads, codes, scales):
    nc.vector.quantize_mx(
        out=codes.bitcast(FP8X4), scales=scales, in_=quads[:].rearrange("p n t -> p (n t)")
    )


def tile_recurrentffn_pb_t_kernel(
    tc, x, hidden_state, swiglu, W_u, b_u, gamma_h, beta_h, W_d, b_d, gamma_o, beta_o, out_0, out_1
):
    nc = tc.nc
    x_v = x.rearrange("(p j) d -> p j d", p=P)
    h_v = hidden_state.rearrange("(p j) d -> p j d", p=P)
    s_v = swiglu.rearrange("(p j) d -> p j d", p=P)
    out_v = out_0.rearrange("(p j) d -> p j d", p=P)
    newh_v = out_1.rearrange("(p j) d -> p j d", p=P)

    with ExitStack() as ctx:
        ctx.enter_context(tc.manual_schedule())
        keep = ctx.enter_context(tc.tile_pool(name="keep", bufs=1))
        hold = ctx.enter_context(tc.tile_pool(name="hold", bufs=GROUPS))
        inp = ctx.enter_context(tc.tile_pool(name="inp", bufs=4))
        early = ctx.enter_context(tc.tile_pool(name="early", bufs=2))
        stat = ctx.enter_context(tc.tile_pool(name="stat", bufs=8))
        const = ctx.enter_context(tc.psum_pool(name="const", bufs=1))
        psum = ctx.enter_context(tc.psum_pool(name="psum", bufs=7))

        live = {}

        def group_rows(g):
            return slice(g * SUB, (g + 1) * SUB)

        def load_gate_inputs(g):
            x_sb = inp.tile([P, SUB, D], BF16, bufs=3)
            nc.sync.dma_start(out=x_sb[:], in_=x_v[:, group_rows(g), :])
            h_sb = inp.tile([P, SUB, H], BF16, bufs=6)
            nc.sync.dma_start(out=h_sb[:], in_=h_v[:, group_rows(g), :])
            live["x", g], live["h", g] = x_sb, h_sb

        def load_candidate(g):
            s_sb = inp.tile([P, SUB, H], BF16, bufs=4)
            nc.sync.dma_start(out=s_sb[:], in_=s_v[:, group_rows(g), :])
            live["s", g] = s_sb

        ident = keep.tile([P, P], F32)
        make_identity(nc, ident[:])
        power = keep.tile([P, AHEAD, SUB], F32)
        nc.gpsimd.memset(power[:], -0.5)
        p_sum = keep.tile([P, GROUPS, SUB], F32)
        p_squares = keep.tile([P, GROUPS, SUB], F32)
        p_neg_mean = keep.tile([P, GROUPS, SUB], F32)
        p_rstd = keep.tile([P, GROUPS, SUB], F32)
        p_shift = keep.tile([P, GROUPS, SUB], F32)
        p_var = keep.tile([P, AHEAD, SUB], F32)
        eps_col = keep.tile([P, 1], F32)
        nc.gpsimd.memset(eps_col[:], EPS)
        twice = keep.tile([P, P], BF16)
        nc.gpsimd.tensor_scalar(out=twice[:], in0=ident[:], scalar1=2.0, scalar2=0.0, op0=ALU.mult, op1=ALU.add)

        sigmoid_set = keep.tile([P, 1], F32)
        nc.scalar.activation(out=sigmoid_set[:], in_=eps_col[:], func=ACT.Sigmoid)

        def turn_inputs(g):
            for t in range(SUB):
                xhT = psum.tile([P, 2, 2, P], F32, tag="bank")
                for c, src in enumerate((live["x", g], live["h", g])):
                    src_words = src[:, t, :].bitcast(F32)
                    for u in range(2):
                        nc.tensor.transpose(xhT[:, c, u, :], src_words[:, u : 2 * P : 2], ident[:])
                live["xhT", g, t] = xhT

        prep = ctx.enter_context(tc.tile_pool(name="prep", bufs=1))
        late = ctx.enter_context(tc.tile_pool(name="late", bufs=2))
        load_gate_inputs(0)
        wu_v = W_u.rearrange("(c p t) n -> c p t n", c=2, p=P)
        wu_raw = []
        for c in range(2):
            raw = prep.tile([P, PACK, H], BF16, name="wu_raw%d" % c)
            nc.sync.dma_start(out=raw[:], in_=wu_v[c])
            wu_raw.append(raw)
        load_candidate(0)
        for g in range(1, LOOKAHEAD):
            load_gate_inputs(g)
            load_candidate(g)
        wd_raw = prep.tile([P, PACK, D], BF16)
        nc.sync.dma_start(out=wd_raw[:], in_=W_d.rearrange("(p t) n -> p t n", p=P))
        turn_inputs(0)

        vec_raw = keep.tile([P, 3, 16], BF16)
        for v, vec in enumerate((b_u, gamma_h, beta_h)):
            nc.gpsimd.dma_start(out=vec_raw[:, v, :CHUNKS], in_=vec.rearrange("(p c) -> p c", c=CHUNKS))
        wu_codes = keep.tile([P, 2, H], U32, align_bytes=64)
        wu_scales = keep.tile([P, 2, H], U8, align_bytes=64)
        wu_quads = []
        for c in range(2):
            quads = prep.tile([P, H, PACK], BF16, align_bytes=64, name="wu_quads%d" % c)
            wu_quads.append(quads)
        lay_quads(nc.vector.tensor_copy, wu_quads[0], wu_raw[0], slice(0, H), True)
        lay_quads(nc.vector.tensor_copy, wu_quads[1], wu_raw[1], slice(0, H // 2), True)
        quantise_pass(nc, wu_quads[0], wu_codes[:, 0], wu_scales[:, 0])

        def column(v, m):
            return vec_cols[:, v - 1, m : m + 1]

        vec_cols = keep.tile([P, 2, CHUNKS], F32)
        wd_quads = late.tile([P, D, PACK], BF16, align_bytes=64, bufs=1)
        bd_all = keep.tile([P, D], BF16)
        ones = keep.tile([P, P], BF16)
        first_rows = late.tile([P, 2, D], BF16, bufs=1)

        def load_second_half():
            nc.gpsimd.tensor_copy(out=vec_cols[:], in_=vec_raw[:, 1:, :CHUNKS])
            nc.gpsimd.memset(ones[:], 1.0)
            nc.gpsimd.memset(first_rows[:], 0.0)
            nc.sync.dma_start(out=bd_all[:], in_=b_d.partition_broadcast(P))
            nc.sync.dma_start(out=first_rows[0:1, 0, :], in_=gamma_o.rearrange("(o d) -> o d", o=1))
            nc.sync.dma_start(out=first_rows[0:1, 1, :], in_=beta_o.rearrange("(o d) -> o d", o=1))

        def prepare_second_half():
            wd_codes = keep.tile([P, D], U32, align_bytes=64)
            wd_scales = keep.tile([P, D], U8, align_bytes=64)
            quantise_pass(nc, wd_quads, wd_codes[:], wd_scales[:])
            gain_shift = const.tile([P, 2, D], BF16)
            for v in range(2):
                nc.tensor.matmul(out=gain_shift[:, v, :], lhsT=ones[:], rhs=first_rows[:, v, :], start=True, stop=True)
            live["wd"] = wd_codes, wd_scales
            live["go_all"], live["bo_all"] = gain_shift[:, 0, :], gain_shift[:, 1, :]

        def copy_inputs_out(g):
            xh_quads = early.tile([P, 2 * TOK * PACK], BF16, align_bytes=64)
            xh_words = xh_quads[:].bitcast(F32).rearrange("q (c k u) -> q c k u", c=2, u=2)
            for t in range(SUB):
                nc.scalar.copy(
                    out=xh_words[:, :, t * P : (t + 1) * P, :],
                    in_=live["xhT", g, t][:].rearrange("q c u k -> q c k u"),
                )
            live["xh_quads", g] = xh_quads

        def quantise_inputs(g):
            xh_codes = early.tile([P, 2, TOK], U32, align_bytes=64)
            xh_scales = early.tile([P, 2, TOK], U8, align_bytes=64)
            nc.vector.quantize_mx(
                out=xh_codes[:].rearrange("q c k -> q (c k)").bitcast(FP8X4),
                scales=xh_scales[:].rearrange("q c k -> q (c k)"),
                in_=live["xh_quads", g][:],
            )
            live["xh_codes", g], live["xh_scales", g] = xh_codes, xh_scales

        def gate_matmul(g, banks=range(CHUNKS // CPB)):
            for b in banks:
                zT = psum.tile([P, CPB, TOK], F32, tag="bank")
                for i in range(CPB):
                    m = b * CPB + i
                    for c in range(2):
                        nc.tensor.matmul_mx(
                            out=zT[:, i, :],
                            lhsT=wu_codes[:, c, m * P : (m + 1) * P].bitcast(FP8X4),
                            lhsT_scale=wu_scales[:, c, m * P : (m + 1) * P],
                            rhs=live["xh_codes", g][:, c, :].bitcast(FP8X4),
                            rhs_scale=live["xh_scales", g][:, c, :],
                            start=(c == 0),
                            stop=(c == 1),
                        )
                live["zT", g, b] = zT

        def gate_sigmoid(g):
            uT = early.tile([P, CHUNKS, TOK], F32)
            for b in range(CHUNKS // CPB):
                for i in range(CPB):
                    m = b * CPB + i
                    nc.scalar.activation(
                        out=uT[:, m, :], in_=live["zT", g, b][:, i, :], func=ACT.Sigmoid,
                        bias=vec_raw[:, 0, m : m + 1], scale=1.0,
                    )
            live["uT", g] = uT

        def turn_gate_back(g):
            for t in range(SUB):
                u_ps = psum.tile([P, H], F32, tag="bank")
                for m in range(CHUNKS):
                    nc.tensor.transpose(
                        u_ps[:, m * P : (m + 1) * P], live["uT", g][:, m, t * P : (t + 1) * P], ident[:]
                    )
                live["u", g, t] = u_ps

        def double_state(g):
            h2 = psum.tile([P, SUB, H], BF16, tag="bank")
            for t in range(SUB):
                nc.tensor.matmul(out=h2[:, t, :], lhsT=twice[:], rhs=live["h", g][:, t, :], start=True, stop=True)
            live["h2", g] = h2

        def difference(g):
            diff = early.tile([P, SUB, H], F32, bufs=3)
            engine = nc.vector if g < HEAD else nc.gpsimd
            for t in range(SUB):
                engine.tensor_tensor(
                    out=diff[:, t, :].rearrange("p (c f i) -> p f c i", c=CHUNKS, i=LINE),
                    in0=live["s", g][:, t, :].rearrange("p (f i c) -> p f c i", c=CHUNKS, i=LINE),
                    in1=live["h", g][:, t, :].rearrange("p (f i c) -> p f c i", c=CHUNKS, i=LINE), op=ALU.subtract,
                )
            live["diff", g] = diff

        def blend(g):
            gated = early.tile([P, SUB, H], F32)
            blended = hold.tile([P, SUB, H], F32)
            for t in range(SUB):
                nc.vector.tensor_tensor(
                    out=gated[:, t, :], in0=live["u", g, t][:], in1=live["diff", g][:, t, :], op=ALU.mult
                )
            for t in range(SUB):
                nc.vector.scalar_tensor_tensor(
                    out=blended[:, t, :].rearrange("p (c f) -> p c f", c=CHUNKS),
                    in0=live["h2", g][:, t, :].rearrange("p (f c) -> p c f", c=CHUNKS), scalar=1.0,
                    in1=gated[:, t, :].rearrange("p (c f) -> p c f", c=CHUNKS),
                    op0=ALU.mult, op1=ALU.add, accum_out=p_sum[:, g, t : t + 1],
                )
            live["p", g] = blended

        def squared_deviations(v, total, squares, width):
            for t in range(SUB):
                junk = early.tile([P, width], BF16)
                nc.scalar.activation(
                    out=junk[:], in_=v[:, t, :], func=ACT.Square, bias=total[:, t : t + 1], scale=-float(width),
                    accum_out=squares[:, t : t + 1],
                )

        def blend_variance(g):
            squared_deviations(live["p", g], p_sum[:, g], p_squares[:, g], H)

        def negative_mean(out, total, width):
            nc.gpsimd.tensor_scalar(out=out, in0=total, scalar1=-1.0 / width, scalar2=0.0, op0=ALU.mult, op1=ALU.add)

        def blend_means(first, end):
            negative_mean(p_neg_mean[:, first:end], p_sum[:, first:end], H)

        def blend_shifts(first, end):
            groups = slice(first, end)
            nc.gpsimd.tensor_tensor(
                out=p_shift[:, groups], in0=p_neg_mean[:, groups], in1=p_rstd[:, groups], op=ALU.mult
            )

        def blend_powers():
            groups = slice(0, AHEAD)
            nc.gpsimd.tensor_scalar(
                out=p_var[:], in0=p_squares[:, groups], scalar1=1.0 / H**3, scalar2=EPS, op0=ALU.mult, op1=ALU.add
            )
            nc.gpsimd.tensor_tensor(out=p_rstd[:, groups], in0=p_var[:], in1=power[:], op=ALU.pow)
            blend_shifts(0, AHEAD)

        def inverse_deviation(out, squares, width):
            nc.scalar.activation(
                out=out, in_=squares, func=ACT.Abs_reciprocal_sqrt, scale=1.0 / width**3, bias=eps_col[:]
            )

        def blend_scales(first, end):
            inverse_deviation(p_rstd[:, first:end], p_squares[:, first:end], H)

        def normalise(g):
            normed = late.tile([P, SUB, H], F32)
            for t in range(SUB):
                nc.gpsimd.tensor_scalar(
                    out=normed[:, t, :], in0=live["p", g][:, t, :],
                    scalar1=p_rstd[:, g, t : t + 1], scalar2=p_shift[:, g, t : t + 1],
                    op0=ALU.mult, op1=ALU.add,
                )
            live["normed", g] = normed

        def turn_normed(g):
            for b in range(CHUNKS // CPB):
                nT = psum.tile([P, CPB, TOK], F32, tag="bank")
                for i in range(CPB):
                    m = b * CPB + i
                    for t in range(SUB):
                        nc.tensor.transpose(
                            nT[:, i, t * P : (t + 1) * P], live["normed", g][:, t, m * P : (m + 1) * P], ident[:]
                        )
                live["nT", g, b] = nT

        def apply_gain(g):
            nhT = late.tile([P, CHUNKS, TOK], F32, bufs=4)
            for b in range(CHUNKS // CPB):
                for i in range(CPB):
                    m = b * CPB + i
                    nc.scalar.activation(
                        out=nhT[:, m, :], in_=live["nT", g, b][:, i, :], func=ACT.Identity,
                        scale=column(1, m), bias=column(2, m),
                    )
            live["nhT", g] = nhT

        def group_state(g):
            nh_quads = late.tile([P, TOK, PACK], BF16, align_bytes=64, bufs=1)
            nc.gpsimd.tensor_scalar(
                out=nh_quads[:].rearrange("j (k i) m -> j k m i", i=LINE),
                in0=live["nhT", g][:].rearrange("j m (k i) -> j k m i", i=LINE),
                scalar1=1.0, scalar2=0.0, op0=ALU.mult, op1=ALU.add,
            )
            live["nh_quads", g] = nh_quads

        def quantise_state(g):
            nh_codes = late.tile([P, TOK], U32, align_bytes=64)
            nh_scales = late.tile([P, TOK], U8, align_bytes=64)
            nc.vector.quantize_mx(
                out=nh_codes[:].bitcast(FP8X4), scales=nh_scales[:],
                in_=live["nh_quads", g][:].rearrange("j k m -> j (k m)"),
            )
            live["nh_codes", g], live["nh_scales", g] = nh_codes, nh_scales

        def turn_state_back(g):
            for t in range(SUB):
                nh_ps = psum.tile([P, H], F32, tag="bank")
                for m in range(CHUNKS):
                    nc.tensor.transpose(
                        nh_ps[:, m * P : (m + 1) * P], live["nhT", g][:, m, t * P : (t + 1) * P], ident[:]
                    )
                live["nh", g, t] = nh_ps

        def store_state(g):
            nh_rows = late.tile([P, SUB, H], F32)
            for t in range(SUB):
                nc.scalar.copy(
                    out=nh_rows[:, t, :].rearrange("p (f c) -> p f c", c=CHUNKS),
                    in_=live["nh", g, t][:].rearrange("p (c f) -> p f c", c=CHUNKS),
                )
                nc.sync.dma_start(out=newh_v[:, g * SUB + t, :], in_=nh_rows[:, t, :])

        def output_matmul(g):
            wd_codes, wd_scales = live["wd"]
            for t in range(SUB):
                y_ps = psum.tile([P, D], F32, tag="bank")
                nc.tensor.matmul_mx(
                    out=y_ps[:],
                    lhsT=live["nh_codes", g][:, t * P : (t + 1) * P].bitcast(FP8X4),
                    lhsT_scale=live["nh_scales", g][:, t * P : (t + 1) * P],
                    rhs=wd_codes[:].bitcast(FP8X4),
                    rhs_scale=wd_scales[:],
                    start=True,
                    stop=True,
                )
                live["y", g, t] = y_ps

        def add_bias(g):
            biased = late.tile([P, SUB, D], F32, bufs=3)
            sum_y = stat.tile([P, SUB], F32)
            for t in range(SUB):
                nc.vector.scalar_tensor_tensor(
                    out=biased[:, t, :], in0=live["y", g, t][:], scalar=1.0, in1=bd_all[:],
                    op0=ALU.mult, op1=ALU.add, accum_out=sum_y[:, t : t + 1],
                )
            live["yb", g], live["sum_y", g] = biased, sum_y

        def output_mean(g):
            y_neg_mean = stat.tile([P, SUB], F32)
            negative_mean(y_neg_mean[:], live["sum_y", g][:], D)
            live["y_neg_mean", g] = y_neg_mean

        def output_variance(g):
            y_squares = stat.tile([P, SUB], F32)
            squared_deviations(live["yb", g], live["sum_y", g], y_squares, D)
            live["y_squares", g] = y_squares

        def output_scale(g):
            y_rstd = stat.tile([P, SUB], F32)
            inverse_deviation(y_rstd[:], live["y_squares", g][:], D)
            live["y_rstd", g] = y_rstd

        def output_gain(g):
            gained = late.tile([P, SUB, D], F32)
            for t in range(SUB):
                nc.vector.scalar_tensor_tensor(
                    out=gained[:, t, :], in0=live["yb", g][:, t, :], scalar=live["y_neg_mean", g][:, t : t + 1],
                    in1=live["go_all"], op0=ALU.add, op1=ALU.mult,
                )
            live["gained", g] = gained

        def output_shift(g):
            out_rows = late.tile([P, SUB, D], F32)
            for t in range(SUB):
                nc.vector.scalar_tensor_tensor(
                    out=out_rows[:, t, :], in0=live["gained", g][:, t, :], scalar=live["y_rstd", g][:, t : t + 1],
                    in1=live["bo_all"], op0=ALU.mult, op1=ALU.add,
                )
                nc.sync.dma_start(out=out_v[:, g * SUB + t, :], in_=out_rows[:, t, :])

        def on(stage, g):
            if 0 <= g < GROUPS:
                stage(g)

        for s in range(SECOND + GROUPS + 4):
            r = s - SECOND
            if s == GROUPS // 2:
                load_second_half()
            on(load_gate_inputs, s + LOOKAHEAD)
            on(load_candidate, s + LOOKAHEAD)
            if s == AHEAD + 3:
                blend_means(0, AHEAD)
                blend_powers()
            if s == GROUPS:
                blend_means(AHEAD, GROUPS - 3)
            if s == GROUPS + 3:
                blend_means(GROUPS - 3, GROUPS)
            on(turn_gate_back, s - 2)
            on(double_state, s - 2)
            on(gate_matmul, s - 1)
            on(turn_inputs, s + 1)
            on(copy_inputs_out, s)
            if s == 0:
                lay_quads(nc.scalar.copy, wu_quads[1], wu_raw[1], slice(H // 2, H), True)
            on(difference, s)
            on(blend, s - 2)
            on(quantise_inputs, s)
            if s == 0:
                quantise_pass(nc, wu_quads[1], wu_codes[:, 1], wu_scales[:, 1])
            if s == 1:
                lay_quads(nc.vector.tensor_copy, wd_quads, wd_raw, slice(0, D), False)
            on(gate_sigmoid, s - 1)

            if r == 0:
                prepare_second_half()
            if s == GROUPS:
                blend_scales(AHEAD, GROUPS - 3)
            if s == GROUPS + 3:
                blend_scales(GROUPS - 3, GROUPS)
            on(output_scale, r - 4)
            on(normalise, r)
            if s == GROUPS:
                blend_shifts(AHEAD, GROUPS - 3)
            if s == GROUPS + 3:
                blend_shifts(GROUPS - 3, GROUPS)
            on(quantise_state, r - 2)
            on(output_matmul, r - 2)
            on(output_mean, r - 3)
            on(apply_gain, r - 1)
            on(blend_variance, s - 3)
            on(output_shift, r - 4)
            on(turn_normed, r)
            on(group_state, r - 1)
            on(store_state, r - 3)
            on(add_bias, r - 2)
            on(turn_state_back, r - 2)
            on(output_variance, r - 3)
            on(output_gain, r - 3)
